import numpy as np
import ml_dtypes


def mxq(x, axis, fmt="e4m3"):
    dtype, down = {"e4m3": (ml_dtypes.float8_e4m3fn, 7), "e5m2": (ml_dtypes.float8_e5m2, 14)}[fmt]
    v = np.moveaxis(np.asarray(x, np.float32).astype(ml_dtypes.bfloat16).astype(np.float64), axis, -1)
    blocks = v.reshape(v.shape[:-1] + (-1, 32))
    amax = np.abs(blocks).max(-1, keepdims=True)
    byte = np.maximum(np.where(amax > 0, np.frexp(amax)[1] - 1 + 127, 0) - down, 1)
    scale = np.exp2(byte - 127.0)
    codes = (blocks / scale).astype(np.float32).astype(dtype).astype(np.float64)
    return np.moveaxis((codes * scale).reshape(v.shape), -1, axis)


WIDE = False


def mx_kscale(k):
    if not WIDE:
        return np.ones(k)
    levels = np.array([10, -10, 5, -5, 0])
    a = np.random.permutation(np.resize(levels, k // 512 * 4)).reshape(k // 512, 4)
    idx = np.arange(k)
    return np.exp2(a[idx // 512, idx % 128 // 32])


BF16 = ml_dtypes.bfloat16


def bf(x):
    return np.asarray(x, np.float32).astype(BF16)


def f64(x):
    return np.asarray(x).astype(np.float64)


B, S, A, D, V, KS, KM, KF = 4, 1024, 16, 512, 512, 1024, 512, 512


def erf(v):
    z = np.clip(v, -6.0, 6.0)
    zz = 2.0 * z * z
    term = z.copy()
    total = z.copy()
    for n in range(1, 120):
        term = term * zz / (2.0 * n + 1.0)
        total = total + term
    return 2.0 / np.sqrt(np.pi) * np.exp(-z * z) * total


def gelu(v):
    return 0.5 * v * (1.0 + erf(v / np.sqrt(2.0)))


def sigmoid(v):
    return 1.0 / (1.0 + np.exp(-v))


def setup_inputs():
    s = mx_kscale(D)
    rn = np.random.standard_normal
    return {"hidden_states": bf(rn((B, S, D)) * s),
            "logits": bf(rn((B, S, V))),
            "W_f1": bf(rn((D, KF)) / np.sqrt(D) / s[:, None]),
            "b_f1": bf(rn(KF) * 0.5),
            "W_f2": bf(rn((KF, V)) * 2.5 / np.sqrt(KF)),
            "b_f2": bf(rn(V) * 0.5)}


def reference(hidden_states, logits, W_f1, b_f1, W_f2, b_f2):
    hid_f = gelu((mxq(f64(hidden_states), 2, "e4m3") @ mxq(f64(W_f1), 0, "e4m3")) + f64(b_f1))
    focus = sigmoid((mxq(hid_f, 2, "e4m3") @ mxq(f64(W_f2), 0, "e4m3")) + f64(b_f2))
    return f64(logits) * (1.0 + focus)

@@ -1,0 +1,260 @@
+from contextlib import ExitStack
+
+import concourse.mybir as mybir
+from concourse.masks import make_identity
+
+FLOPS = 2 * 4096 * 512 * 512 * 2
+
+BF16 = mybir.dt.bfloat16
+F32 = mybir.dt.float32
+U32 = mybir.dt.uint32
+U8 = mybir.dt.uint8
+FP8X4 = mybir.dt.float8_e4m3fn_x4
+ACT = mybir.ActivationFunctionType
+ALU = mybir.AluOpType
+
+P = 128
+NCH = 8
+TPC = 4
+PINNED = True
+
+
+def tile_sparseoutputprojection_pb_t_kernel(tc, hidden_states, logits, W_f1, b_f1, W_f2, b_f2, out):
+    nc = tc.nc
+    hv = hidden_states.flatten_outer_dims().rearrange("(p n) d -> p n d", n=32)
+    lv = logits.flatten_outer_dims().rearrange("(p n) d -> p n d", n=32)
+    ov = out.flatten_outer_dims().rearrange("(p n) d -> p n d", n=32)
+
+    with ExitStack() as ctx:
+        consts = ctx.enter_context(tc.tile_pool(name="consts", bufs=1))
+        work = ctx.enter_context(tc.tile_pool(name="work", bufs=3))
+        ps_a = ctx.enter_context(tc.psum_pool(name="psa", bufs=4))
+        ps_b = ctx.enter_context(tc.psum_pool(name="psb", bufs=4))
+        if PINNED:
+            ctx.enter_context(tc.manual_schedule())
+
+        ident = consts.tile([P, P], F32, name="ident")
+        warm = consts.tile([P, 1], F32, name="warm")
+        warm2 = consts.tile([P, 1], F32, name="warm2")
+        braw = consts.tile([P, P], BF16, name="braw")
+        bf32 = consts.tile([P, P], F32, name="bf32")
+        bias_sb = consts.tile([P, 8], F32, name="bias_sb")
+        wraw = {}
+        wgrp = {}
+        wcod = {}
+        wscl = {}
+        for s in range(2):
+            wraw[s] = consts.tile([P, 4, 512], BF16, name="wraw%d" % s)
+            wgrp[s] = consts.tile([P, 2048], BF16, name="wgrp%d" % s, align_bytes=64)
+            wcod[s] = consts.tile([P, 512], U32, name="wcod%d" % s, align_bytes=64)
+            wscl[s] = consts.tile([P, 512], U8, name="wscl%d" % s, align_bytes=64)
+        h_sb = {}
+        lg_sb = {}
+        h2c = {}
+        h2s = {}
+        for c in range(NCH):
+            h_sb[c] = consts.tile([P, 2048], BF16, name="h_sb%d" % c)
+            lg_sb[c] = consts.tile([P, 2048], BF16, name="lg_sb%d" % c)
+            h2c[c] = consts.tile([P, 512], U32, name="h2c%d" % c, align_bytes=64)
+            h2s[c] = consts.tile([P, 512], U8, name="h2s%d" % c, align_bytes=64)
+
+        nc.vector.memset(warm[:], 0.0)
+        nc.vector.memset(braw[:], 0.0)
+        nc.scalar.dma_start(out=braw[0:4, :], in_=b_f1.rearrange("(t p) -> t p", p=P))
+        nc.scalar.dma_start(out=braw[4:8, :], in_=b_f2.rearrange("(t p) -> t p", p=P))
+        nc.scalar.activation(out=warm2[:], in_=warm[:], func=ACT.Gelu)
+        make_identity(nc, ident[:])
+
+        def load_w1():
+            for u in range(2):
+                nc.sync.dma_start(
+                    out=wraw[0][:, 2 * u : 2 * u + 2, :],
+                    in_=W_f1[256 * u : 256 * u + 256, :].rearrange("(q e) c -> q e c", e=2),
+                )
+
+        def load_h(c):
+            nc.sync.dma_start(
+                out=h_sb[c][:].rearrange("p (n d) -> p n d", n=TPC),
+                in_=hv[:, TPC * c : TPC * c + TPC, :],
+            )
+
+        load_w1()
+        load_h(0)
+        load_h(1)
+        load_h(2)
+        nc.sync.dma_start(out=wraw[1][:], in_=W_f2.rearrange("(t p) v -> p t v", p=P))
+        for c in range(3, NCH):
+            load_h(c)
+        for c in range(NCH):
+            nc.sync.dma_start(
+                out=lg_sb[c][:].rearrange("p (n d) -> p n d", n=TPC),
+                in_=lv[:, TPC * c : TPC * c + TPC, :],
+            )
+
+        def w_regroup(s):
+            nc.vector.tensor_copy(
+                out=wgrp[s][:].rearrange("p (c i t) -> p c t i", i=4, t=4),
+                in_=wraw[s][:].rearrange("p t (c i) -> p c t i", i=4),
+            )
+
+        def w_quant(s):
+            nc.vector.quantize_mx(out=wcod[s][:].bitcast(FP8X4), scales=wscl[s][:], in_=wgrp[s][:])
+
+        nc.vector.tensor_copy(out=bf32[:], in_=braw[:])
+        bps = ps_b.tile([P, P], F32, name="bps", tag="B")
+        nc.tensor.transpose(bps[:], bf32[:], ident[:])
+
+        xts = {}
+        grps = {}
+        hcs = {}
+        hss = {}
+        ps1 = {}
+        hidp = {}
+        hgs = {}
+        ps2 = {}
+        fts = {}
+        fbs = {}
+        osb = {}
+
+        def st_a(c):
+            hw = h_sb[c][:].bitcast(F32)
+            for b in range(2):
+                xt = ps_a.tile([P, 2, 256], F32, name="xt%d_%d" % (c, b), tag="A")
+                xts[(c, b)] = xt
+                for a2 in range(2):
+                    for u in range(2):
+                        col = 256 * (2 * b + a2) + 128 * u
+                        nc.tensor.transpose(xt[:, u, 128 * a2 : 128 * a2 + 128], hw[:, col : col + 128], ident[:])
+
+        def st_b(c):
+            grp = work.tile([P, 2048], BF16, name="grp%d" % c, tag="grp", align_bytes=64)
+            grps[c] = grp
+            gw = grp[:].bitcast(F32)
+            for b in range(2):
+                dst = gw[:, 512 * b : 512 * b + 512].rearrange("p (n u) -> p n u", u=2)
+                src = xts[(c, b)][:].rearrange("p u n -> p n u")
+                if b == 0:
+                    nc.vector.tensor_copy(out=dst, in_=src)
+                else:
+                    nc.scalar.copy(out=dst, in_=src)
+
+        def st_c(c):
+            hcs[c] = work.tile([P, 512], U32, name="hc%d" % c, tag="hc", align_bytes=64)
+            hss[c] = work.tile([P, 512], U8, name="hs%d" % c, tag="hs", align_bytes=64)
+            nc.vector.quantize_mx(out=hcs[c][:].bitcast(FP8X4), scales=hss[c][:], in_=grps[c][:])
+
+        def st_d(c, m):
+            ps = ps_b.tile([P, 512], F32, name="ps1_%d_%d" % (c, m), tag="B")
+            ps1[(c, m)] = ps
+            nc.tensor.matmul_mx(
+                out=ps[:],
+                lhsT=wcod[0][:, 128 * m : 128 * m + 128].bitcast(FP8X4),
+                lhsT_scale=wscl[0][:, 128 * m : 128 * m + 128],
+                rhs=hcs[c][:].bitcast(FP8X4),
+                rhs_scale=hss[c][:],
+                start=True,
+                stop=True,
+            )
+
+        def st_e(c, m):
+            if m == 0:
+                hidp[c] = work.tile([P, 4, 512], BF16, name="hidp%d" % c, tag="hidp")
+            nc.scalar.activation(
+                out=hidp[c][:, m, :], in_=ps1[(c, m)][:], func=ACT.Gelu, bias=bias_sb[:, m : m + 1], scale=1.0
+            )
+
+        def st_f(c):
+            hgs[c] = work.tile([P, 2048], BF16, name="hg%d" % c, tag="hg", align_bytes=64)
+            nc.vector.tensor_copy(
+                out=hgs[c][:].rearrange("p (c i t) -> p c t i", i=4, t=4),
+                in_=hidp[c][:].rearrange("p t (c i) -> p c t i", i=4),
+            )
+
+        def st_g(c):
+            nc.vector.quantize_mx(out=h2c[c][:].bitcast(FP8X4), scales=h2s[c][:], in_=hgs[c][:])
+
+        def st_h(c, j):
+            ps = ps_a.tile([P, 512], F32, name="ps2_%d_%d" % (c, j), tag="A")
+            ps2[(c, j)] = ps
+            nc.tensor.matmul_mx(
+                out=ps[:],
+                lhsT=wcod[1][:, 128 * j : 128 * j + 128].bitcast(FP8X4),
+                lhsT_scale=wscl[1][:, 128 * j : 128 * j + 128],
+                rhs=h2c[c][:].bitcast(FP8X4),
+                rhs_scale=h2s[c][:],
+                start=True,
+                stop=True,
+            )
+
+        def st_i(c, j):
+            if j == 0:
+                fts[c] = work.tile([P, 4, 512], F32, name="ft%d" % c, tag="ft")
+            nc.scalar.activation(
+                out=fts[c][:, j, :], in_=ps2[(c, j)][:], func=ACT.Sigmoid, bias=bias_sb[:, 4 + j : 5 + j], scale=1.0
+            )
+
+        def st_j(c, a):
+            fb = ps_b.tile([P, 512], F32, name="fb%d_%d" % (c, a), tag="B")
+            fbs[(c, a)] = fb
+            for j in range(4):
+                nc.tensor.transpose(fb[:, 128 * j : 128 * j + 128], fts[c][:, j, 128 * a : 128 * a + 128], ident[:])
+
+        def st_k(c, a):
+            if a == 0:
+                osb[c] = work.tile([P, 4, 512], F32, name="osb%d" % c, tag="osb")
+            nc.vector.scalar_tensor_tensor(
+                out=osb[c][:, a, :],
+                in0=fbs[(c, a)][:],
+                scalar=1.0,
+                in1=lg_sb[c][:, 512 * a : 512 * a + 512],
+                op0=ALU.add,
+                op1=ALU.mult,
+            )
+
+        def ok(c):
+            return 0 <= c < NCH
+
+        for i in range(-3, NCH + 1):
+            if i == 7:
+                for j in range(4):
+                    st_h(0, j)
+            if ok(i + 3):
+                st_a(i + 3)
+            if i == -3:
+                w_regroup(0)
+                nc.vector.tensor_copy(out=bias_sb[:], in_=bps[:, 0:8])
+            if ok(i + 2):
+                st_b(i + 2)
+            if ok(i - 1):
+                st_f(i - 1)
+            if i == -2:
+                w_quant(0)
+            if i == 6:
+                w_regroup(1)
+            if ok(i + 2):
+                st_c(i + 2)
+            if ok(i - 1):
+                st_g(i - 1)
+            if i == 6:
+                w_quant(1)
+            for m in range(4):
+                if ok(i):
+                    st_e(i, m)
+                if ok(i + 1):
+                    st_d(i + 1, m)
+
+        for i in range(0, NCH + 1):
+            c = i - 1
+            if ok(c):
+                for a in range(TPC):
+                    st_j(c, a)
+                    st_k(c, a)
+                    if c == NCH - 1:
+                        nc.sync.dma_start(out=ov[:, TPC * c + a, :], in_=osb[c][:, a, :])
+                if c < NCH - 1:
+                    nc.sync.dma_start(out=ov[:, TPC * c : TPC * c + TPC, :], in_=osb[c][:])
+            for j in range(4):
+                if ok(i):
+                    st_i(i, j)
+                if ok(i + 1):
+                    st_h(i + 1, j)

@@ -60,8 +60,6 @@ def tile_sparseoutputprojection_pb_t_kernel(tc, hidden_states, logits, W_f1, b_f
 
         nc.vector.memset(warm[:], 0.0)
         nc.vector.memset(braw[:], 0.0)
-        nc.scalar.dma_start(out=braw[0:4, :], in_=b_f1.rearrange("(t p) -> t p", p=P))
-        nc.scalar.dma_start(out=braw[4:8, :], in_=b_f2.rearrange("(t p) -> t p", p=P))
         nc.scalar.activation(out=warm2[:], in_=warm[:], func=ACT.Gelu)
         make_identity(nc, ident[:])
 
@@ -72,14 +70,17 @@ def tile_sparseoutputprojection_pb_t_kernel(tc, hidden_states, logits, W_f1, b_f
                     in_=W_f1[256 * u : 256 * u + 256, :].rearrange("(q e) c -> q e c", e=2),
                 )
 
-        def load_h(c):
+        def load_h(c, n0=0, nn=TPC):
             nc.sync.dma_start(
-                out=h_sb[c][:].rearrange("p (n d) -> p n d", n=TPC),
-                in_=hv[:, TPC * c : TPC * c + TPC, :],
+                out=h_sb[c][:, 512 * n0 : 512 * (n0 + nn)].rearrange("p (n d) -> p n d", n=nn),
+                in_=hv[:, TPC * c + n0 : TPC * c + n0 + nn, :],
             )
 
         load_w1()
-        load_h(0)
+        nc.sync.dma_start(out=braw[0:4, :], in_=b_f1.rearrange("(t p) -> t p", p=P))
+        nc.sync.dma_start(out=braw[4:8, :], in_=b_f2.rearrange("(t p) -> t p", p=P))
+        load_h(0, 0, 2)
+        load_h(0, 2, 2)
         load_h(1)
         load_h(2)
         nc.sync.dma_start(out=wraw[1][:], in_=W_f2.rearrange("(t p) v -> p t v", p=P))
@@ -100,9 +101,7 @@ def tile_sparseoutputprojection_pb_t_kernel(tc, hidden_states, logits, W_f1, b_f
         def w_quant(s):
             nc.vector.quantize_mx(out=wcod[s][:].bitcast(FP8X4), scales=wscl[s][:], in_=wgrp[s][:])
 
-        nc.vector.tensor_copy(out=bf32[:], in_=braw[:])
         bps = ps_b.tile([P, P], F32, name="bps", tag="B")
-        nc.tensor.transpose(bps[:], bf32[:], ident[:])
 
         xts = {}
         grps = {}
@@ -133,10 +132,10 @@ def tile_sparseoutputprojection_pb_t_kernel(tc, hidden_states, logits, W_f1, b_f
             for b in range(2):
                 dst = gw[:, 512 * b : 512 * b + 512].rearrange("p (n u) -> p n u", u=2)
                 src = xts[(c, b)][:].rearrange("p u n -> p n u")
-                if b == 0:
-                    nc.vector.tensor_copy(out=dst, in_=src)
-                else:
+                if b == 1 and c <= 5:
                     nc.scalar.copy(out=dst, in_=src)
+                else:
+                    nc.vector.tensor_copy(out=dst, in_=src)
 
         def st_c(c):
             hcs[c] = work.tile([P, 512], U32, name="hc%d" % c, tag="hc", align_bytes=64)
@@ -158,13 +157,13 @@ def tile_sparseoutputprojection_pb_t_kernel(tc, hidden_states, logits, W_f1, b_f
 
         def st_e(c, m):
             if m == 0:
-                hidp[c] = work.tile([P, 4, 512], BF16, name="hidp%d" % c, tag="hidp")
+                hidp[c] = work.tile([P, 4, 512], BF16, name="hidp%d" % c, tag="hidp", bufs=6)
             nc.scalar.activation(
                 out=hidp[c][:, m, :], in_=ps1[(c, m)][:], func=ACT.Gelu, bias=bias_sb[:, m : m + 1], scale=1.0
             )
 
         def st_f(c):
-            hgs[c] = work.tile([P, 2048], BF16, name="hg%d" % c, tag="hg", align_bytes=64)
+            hgs[c] = work.tile([P, 2048], BF16, name="hg%d" % c, tag="hg", bufs=2, align_bytes=64)
             nc.vector.tensor_copy(
                 out=hgs[c][:].rearrange("p (c i t) -> p c t i", i=4, t=4),
                 in_=hidp[c][:].rearrange("p t (c i) -> p c t i", i=4),
@@ -214,6 +213,7 @@ def tile_sparseoutputprojection_pb_t_kernel(tc, hidden_states, logits, W_f1, b_f
         def ok(c):
             return 0 <= c < NCH
 
+        fg_slot = {1: [0], 2: [1], 3: [2], 4: [3], 6: [4], 7: [5], 8: [6, 7]}
         for i in range(-3, NCH + 1):
             if i == 7:
                 for j in range(4):
@@ -222,19 +222,22 @@ def tile_sparseoutputprojection_pb_t_kernel(tc, hidden_states, logits, W_f1, b_f
                 st_a(i + 3)
             if i == -3:
                 w_regroup(0)
-                nc.vector.tensor_copy(out=bias_sb[:], in_=bps[:, 0:8])
+                nc.vector.tensor_copy(out=bf32[:], in_=braw[:])
+                nc.tensor.transpose(bps[:], bf32[:], ident[:])
+                w_quant(0)
             if ok(i + 2):
                 st_b(i + 2)
-            if ok(i - 1):
-                st_f(i - 1)
-            if i == -2:
-                w_quant(0)
+            fg = fg_slot.get(i, [])
+            for c in fg:
+                st_f(c)
             if i == 6:
                 w_regroup(1)
             if ok(i + 2):
                 st_c(i + 2)
-            if ok(i - 1):
-                st_g(i - 1)
+            if i == -2:
+                nc.vector.tensor_copy(out=bias_sb[:], in_=bps[:, 0:8])
+            for c in fg:
+                st_g(c)
             if i == 6:
                 w_quant(1)
             for m in range(4):
@@ -251,8 +254,8 @@ def tile_sparseoutputprojection_pb_t_kernel(tc, hidden_states, logits, W_f1, b_f
                     st_k(c, a)
                     if c == NCH - 1:
                         nc.sync.dma_start(out=ov[:, TPC * c + a, :], in_=osb[c][:, a, :])
-                if c < NCH - 1:
-                    nc.sync.dma_start(out=ov[:, TPC * c : TPC * c + TPC, :], in_=osb[c][:])
+                    elif a % 2 == 1:
+                        nc.sync.dma_start(out=ov[:, TPC * c + a - 1 : TPC * c + a + 1, :], in_=osb[c][:, a - 1 : a + 1, :])
             for j in range(4):
                 if ok(i):
                     st_i(i, j)

@@ -16,7 +16,7 @@ ALU = mybir.AluOpType
 P = 128
 NCH = 8
 TPC = 4
-PINNED = True
+PINNED = False
 
 
 def tile_sparseoutputprojection_pb_t_kernel(tc, hidden_states, logits, W_f1, b_f1, W_f2, b_f2, out):

@@ -16,7 +16,7 @@ ALU = mybir.AluOpType
 P = 128
 NCH = 8
 TPC = 4
-PINNED = False
+PINNED = True
 
 
 def tile_sparseoutputprojection_pb_t_kernel(tc, hidden_states, logits, W_f1, b_f1, W_f2, b_f2, out):
@@ -132,7 +132,7 @@ def tile_sparseoutputprojection_pb_t_kernel(tc, hidden_states, logits, W_f1, b_f
             for b in range(2):
                 dst = gw[:, 512 * b : 512 * b + 512].rearrange("p (n u) -> p n u", u=2)
                 src = xts[(c, b)][:].rearrange("p u n -> p n u")
-                if b == 1 and c <= 5:
+                if b == 1 and c <= 4:
                     nc.scalar.copy(out=dst, in_=src)
                 else:
                     nc.vector.tensor_copy(out=dst, in_=src)
@@ -213,7 +213,7 @@ def tile_sparseoutputprojection_pb_t_kernel(tc, hidden_states, logits, W_f1, b_f
         def ok(c):
             return 0 <= c < NCH
 
-        fg_slot = {1: [0], 2: [1], 3: [2], 4: [3], 6: [4], 7: [5], 8: [6, 7]}
+        fg_slot = {1: [0], 2: [1], 4: [2], 6: [3], 7: [4, 5], 8: [6, 7]}
         for i in range(-3, NCH + 1):
             if i == 7:
                 for j in range(4):
@@ -230,7 +230,7 @@ def tile_sparseoutputprojection_pb_t_kernel(tc, hidden_states, logits, W_f1, b_f
             fg = fg_slot.get(i, [])
             for c in fg:
                 st_f(c)
-            if i == 6:
+            if i == 0:
                 w_regroup(1)
             if ok(i + 2):
                 st_c(i + 2)
@@ -238,7 +238,7 @@ def tile_sparseoutputprojection_pb_t_kernel(tc, hidden_states, logits, W_f1, b_f
                 nc.vector.tensor_copy(out=bias_sb[:], in_=bps[:, 0:8])
             for c in fg:
                 st_g(c)
-            if i == 6:
+            if i == 0:
                 w_quant(1)
             for m in range(4):
                 if ok(i):

@@ -16,7 +16,15 @@ ALU = mybir.AluOpType
 P = 128
 NCH = 8
 TPC = 4
-PINNED = True
+
+N_TANH = 1
+R_PIECES = 4
+W2_PIECES = 2
+W2_ENG = 0
+S_PROG = "e20 e21 g1 g2 g3 g4 g5 g6 g7 t0 t1 t2 t3 t4 t5 t6 t7a t7b"
+PE_PROG = "h1 M0b h2 M1 h3 M2 h4 M3 h5 M4 h6 M5 h7 M6 M7 X0 X1 o0 X2 o1 X3 o2 X4 o3 X5 o4 X6 o5 X7a o6 X7b o7a o7b"
+V_PROG = "e1 q1 w q2 W e3 q3 e4 q4 e5 q5 e6 q6 e7 q7 k0 k1 r2 r3 H0 r4 k2 k3 p0 k4 p1 k5 p2 k6 p3 k7 p4 p5 p6 p7a p7b"
+G_PROG = "r0 r1 r5 r6 r7"
 
 
 def tile_sparseoutputprojection_pb_t_kernel(tc, hidden_states, logits, W_f1, b_f1, W_f2, b_f2, out):
@@ -28,80 +36,94 @@ def tile_sparseoutputprojection_pb_t_kernel(tc, hidden_states, logits, W_f1, b_f
     with ExitStack() as ctx:
         consts = ctx.enter_context(tc.tile_pool(name="consts", bufs=1))
         work = ctx.enter_context(tc.tile_pool(name="work", bufs=3))
-        ps_a = ctx.enter_context(tc.psum_pool(name="psa", bufs=4))
-        ps_b = ctx.enter_context(tc.psum_pool(name="psb", bufs=4))
-        if PINNED:
-            ctx.enter_context(tc.manual_schedule())
+        ps_m = ctx.enter_context(tc.psum_pool(name="psm", bufs=4))
+        ps_t = ctx.enter_context(tc.psum_pool(name="pst", bufs=4))
+        ctx.enter_context(tc.manual_schedule())
 
         ident = consts.tile([P, P], F32, name="ident")
         warm = consts.tile([P, 1], F32, name="warm")
         warm2 = consts.tile([P, 1], F32, name="warm2")
         braw = consts.tile([P, P], BF16, name="braw")
         bf32 = consts.tile([P, P], F32, name="bf32")
-        bias_sb = consts.tile([P, 8], F32, name="bias_sb")
+        bias_sb = consts.tile([P, 12], F32, name="bias_sb")
         wraw = {}
         wgrp = {}
         wcod = {}
         wscl = {}
         for s in range(2):
             wraw[s] = consts.tile([P, 4, 512], BF16, name="wraw%d" % s)
-            wgrp[s] = consts.tile([P, 2048], BF16, name="wgrp%d" % s, align_bytes=64)
-            wcod[s] = consts.tile([P, 512], U32, name="wcod%d" % s, align_bytes=64)
-            wscl[s] = consts.tile([P, 512], U8, name="wscl%d" % s, align_bytes=64)
+            for hf in range(2):
+                wgrp[(s, hf)] = consts.tile([P, 1024], BF16, name="wgrp%d_%d" % (s, hf), align_bytes=64)
+                wcod[(s, hf)] = consts.tile([P, 256], U32, name="wcod%d_%d" % (s, hf), align_bytes=64)
+                wscl[(s, hf)] = consts.tile([P, 256], U8, name="wscl%d_%d" % (s, hf), align_bytes=64)
         h_sb = {}
         lg_sb = {}
-        h2c = {}
-        h2s = {}
         for c in range(NCH):
-            h_sb[c] = consts.tile([P, 2048], BF16, name="h_sb%d" % c)
             lg_sb[c] = consts.tile([P, 2048], BF16, name="lg_sb%d" % c)
-            h2c[c] = consts.tile([P, 512], U32, name="h2c%d" % c, align_bytes=64)
-            h2s[c] = consts.tile([P, 512], U8, name="h2s%d" % c, align_bytes=64)
 
         nc.vector.memset(warm[:], 0.0)
         nc.vector.memset(braw[:], 0.0)
         nc.scalar.activation(out=warm2[:], in_=warm[:], func=ACT.Gelu)
         make_identity(nc, ident[:])
 
-        def load_w1():
-            for u in range(2):
-                nc.sync.dma_start(
-                    out=wraw[0][:, 2 * u : 2 * u + 2, :],
-                    in_=W_f1[256 * u : 256 * u + 256, :].rearrange("(q e) c -> q e c", e=2),
-                )
-
         def load_h(c, n0=0, nn=TPC):
+            if n0 == 0:
+                h_sb[c] = work.tile([P, 2048], BF16, name="h_sb%d" % c, tag="h_sb", bufs=7)
             nc.sync.dma_start(
                 out=h_sb[c][:, 512 * n0 : 512 * (n0 + nn)].rearrange("p (n d) -> p n d", n=nn),
                 in_=hv[:, TPC * c + n0 : TPC * c + n0 + nn, :],
             )
 
-        load_w1()
-        nc.sync.dma_start(out=braw[0:4, :], in_=b_f1.rearrange("(t p) -> t p", p=P))
-        nc.sync.dma_start(out=braw[4:8, :], in_=b_f2.rearrange("(t p) -> t p", p=P))
-        load_h(0, 0, 2)
-        load_h(0, 2, 2)
-        load_h(1)
-        load_h(2)
-        nc.sync.dma_start(out=wraw[1][:], in_=W_f2.rearrange("(t p) v -> p t v", p=P))
-        for c in range(3, NCH):
-            load_h(c)
-        for c in range(NCH):
+        def load_lg(c):
             nc.sync.dma_start(
                 out=lg_sb[c][:].rearrange("p (n d) -> p n d", n=TPC),
                 in_=lv[:, TPC * c : TPC * c + TPC, :],
             )
 
-        def w_regroup(s):
-            nc.vector.tensor_copy(
-                out=wgrp[s][:].rearrange("p (c i t) -> p c t i", i=4, t=4),
-                in_=wraw[s][:].rearrange("p t (c i) -> p c t i", i=4),
+        def load_w1(u):
+            nc.sync.dma_start(
+                out=wraw[0][:, 2 * u : 2 * u + 2, :],
+                in_=W_f1[256 * u : 256 * u + 256, :].rearrange("(q e) c -> q e c", e=2),
             )
 
-        def w_quant(s):
-            nc.vector.quantize_mx(out=wcod[s][:].bitcast(FP8X4), scales=wscl[s][:], in_=wgrp[s][:])
+        load_h(0, 0, 2)
+        nc.sync.dma_start(out=braw[0:4, :], in_=b_f1.rearrange("(t p) -> t p", p=P))
+        nc.sync.dma_start(out=braw[4:8, :], in_=b_f2.rearrange("(t p) -> t p", p=P))
+        load_w1(0)
+        load_w1(1)
+        load_h(0, 2, 2)
+        load_h(1)
+        load_h(2)
+        nc.sync.dma_start(out=wraw[1][:], in_=W_f2.rearrange("(t p) v -> p t v", p=P))
+        load_h(3)
+        load_h(4)
+        load_h(5)
 
-        bps = ps_b.tile([P, P], F32, name="bps", tag="B")
+        def w_regroup(s, hf, eng):
+            dst = wgrp[(s, hf)][:].rearrange("p (c i t) -> p c t i", i=4, t=4)
+            src = wraw[s][:, :, 256 * hf : 256 * hf + 256].rearrange("p t (c i) -> p c t i", i=4)
+            if eng == 0:
+                nc.vector.tensor_copy(out=dst, in_=src)
+            elif eng == 1:
+                nc.scalar.copy(out=dst, in_=src)
+            else:
+                w = 256 // W2_PIECES
+                for r in range(W2_PIECES):
+                    nc.gpsimd.tensor_scalar(
+                        out=wgrp[(s, hf)][:, 4 * w * r : 4 * w * (r + 1)].rearrange("p (c i t) -> p c t i", i=4, t=4),
+                        in0=wraw[s][:, :, 256 * hf + w * r : 256 * hf + w * (r + 1)].rearrange("p t (c i) -> p c t i", i=4),
+                        scalar1=1.0,
+                        scalar2=0.0,
+                        op0=ALU.mult,
+                        op1=ALU.add,
+                    )
+
+        def w_quant(s, hf):
+            nc.vector.quantize_mx(out=wcod[(s, hf)][:].bitcast(FP8X4), scales=wscl[(s, hf)][:], in_=wgrp[(s, hf)][:])
+
+        def w_col(s, m):
+            lo = 128 * (m % 2)
+            return wcod[(s, m // 2)][:, lo : lo + 128].bitcast(FP8X4), wscl[(s, m // 2)][:, lo : lo + 128]
 
         xts = {}
         grps = {}
@@ -110,154 +132,274 @@ def tile_sparseoutputprojection_pb_t_kernel(tc, hidden_states, logits, W_f1, b_f
         ps1 = {}
         hidp = {}
         hgs = {}
+        h2c = {}
+        h2s = {}
         ps2 = {}
         fts = {}
         fbs = {}
         osb = {}
 
-        def st_a(c):
+        def h_transpose(c, b):
             hw = h_sb[c][:].bitcast(F32)
-            for b in range(2):
-                xt = ps_a.tile([P, 2, 256], F32, name="xt%d_%d" % (c, b), tag="A")
-                xts[(c, b)] = xt
-                for a2 in range(2):
-                    for u in range(2):
-                        col = 256 * (2 * b + a2) + 128 * u
-                        nc.tensor.transpose(xt[:, u, 128 * a2 : 128 * a2 + 128], hw[:, col : col + 128], ident[:])
+            xt = ps_t.tile([P, 2, 256], F32, name="xt%d_%d" % (c, b), tag="T")
+            xts[(c, b)] = xt
+            for a2 in range(2):
+                for u in range(2):
+                    col = 256 * (2 * b + a2) + 128 * u
+                    nc.tensor.transpose(xt[:, u, 128 * a2 : 128 * a2 + 128], hw[:, col : col + 128], ident[:])
 
-        def st_b(c):
-            grp = work.tile([P, 2048], BF16, name="grp%d" % c, tag="grp", align_bytes=64)
-            grps[c] = grp
-            gw = grp[:].bitcast(F32)
-            for b in range(2):
-                dst = gw[:, 512 * b : 512 * b + 512].rearrange("p (n u) -> p n u", u=2)
-                src = xts[(c, b)][:].rearrange("p u n -> p n u")
-                if b == 1 and c <= 4:
-                    nc.scalar.copy(out=dst, in_=src)
-                else:
-                    nc.vector.tensor_copy(out=dst, in_=src)
+        def h_evac(c, b, scalar):
+            if b == 0:
+                grps[c] = work.tile([P, 2048], BF16, name="grp%d" % c, tag="grp", bufs=3, align_bytes=64)
+            dst = grps[c][:].bitcast(F32)[:, 512 * b : 512 * b + 512].rearrange("p (n u) -> p n u", u=2)
+            src = xts[(c, b)][:].rearrange("p u n -> p n u")
+            if scalar:
+                nc.scalar.copy(out=dst, in_=src)
+            else:
+                nc.vector.tensor_copy(out=dst, in_=src)
 
-        def st_c(c):
-            hcs[c] = work.tile([P, 512], U32, name="hc%d" % c, tag="hc", align_bytes=64)
-            hss[c] = work.tile([P, 512], U8, name="hs%d" % c, tag="hs", align_bytes=64)
-            nc.vector.quantize_mx(out=hcs[c][:].bitcast(FP8X4), scales=hss[c][:], in_=grps[c][:])
+        def h_quant(c, t0=0, nt=512):
+            if t0 == 0:
+                hcs[c] = work.tile([P, 512], U32, name="hc%d" % c, tag="hc", bufs=4, align_bytes=64)
+                hss[c] = work.tile([P, 512], U8, name="hs%d" % c, tag="hs", bufs=4, align_bytes=64)
+            nc.vector.quantize_mx(
+                out=hcs[c][:, t0 : t0 + nt].bitcast(FP8X4),
+                scales=hss[c][:, t0 : t0 + nt],
+                in_=grps[c][:, 4 * t0 : 4 * t0 + 4 * nt],
+            )
 
-        def st_d(c, m):
-            ps = ps_b.tile([P, 512], F32, name="ps1_%d_%d" % (c, m), tag="B")
-            ps1[(c, m)] = ps
+        def mx1(c, m, t0=0, nt=512):
+            ps = ps_m.tile([P, 512], F32, name="ps1_%d_%d_%d" % (c, m, t0), tag="M")
+            ps1[(c, m, t0)] = ps
+            w, ws = w_col(0, m)
             nc.tensor.matmul_mx(
-                out=ps[:],
-                lhsT=wcod[0][:, 128 * m : 128 * m + 128].bitcast(FP8X4),
-                lhsT_scale=wscl[0][:, 128 * m : 128 * m + 128],
-                rhs=hcs[c][:].bitcast(FP8X4),
-                rhs_scale=hss[c][:],
+                out=ps[:, 0:nt],
+                lhsT=w,
+                lhsT_scale=ws,
+                rhs=hcs[c][:, t0 : t0 + nt].bitcast(FP8X4),
+                rhs_scale=hss[c][:, t0 : t0 + nt],
                 start=True,
                 stop=True,
             )
 
-        def st_e(c, m):
-            if m == 0:
-                hidp[c] = work.tile([P, 4, 512], BF16, name="hidp%d" % c, tag="hidp", bufs=6)
+        def gelu(c, m, t0=0, nt=512):
+            if m == 0 and t0 == 0:
+                hidp[c] = work.tile([P, 4, 512], BF16, name="hidp%d" % c, tag="hidp", bufs=7)
             nc.scalar.activation(
-                out=hidp[c][:, m, :], in_=ps1[(c, m)][:], func=ACT.Gelu, bias=bias_sb[:, m : m + 1], scale=1.0
+                out=hidp[c][:, m, t0 : t0 + nt],
+                in_=ps1[(c, m, t0)][:, 0:nt],
+                func=ACT.Gelu,
+                bias=bias_sb[:, m : m + 1],
+                scale=1.0,
             )
 
-        def st_f(c):
-            hgs[c] = work.tile([P, 2048], BF16, name="hg%d" % c, tag="hg", bufs=2, align_bytes=64)
-            nc.vector.tensor_copy(
-                out=hgs[c][:].rearrange("p (c i t) -> p c t i", i=4, t=4),
-                in_=hidp[c][:].rearrange("p t (c i) -> p c t i", i=4),
-            )
+        def hid_regroup(c, vec):
+            hgs[c] = work.tile([P, 2048], BF16, name="hg%d" % c, tag="hg", bufs=6, align_bytes=64)
+            if vec:
+                nc.vector.tensor_copy(
+                    out=hgs[c][:].rearrange("p (c i t) -> p c t i", i=4, t=4),
+                    in_=hidp[c][:].rearrange("p t (c i) -> p c t i", i=4),
+                )
+                return
+            w = 512 // R_PIECES
+            for r in range(R_PIECES):
+                nc.gpsimd.tensor_scalar(
+                    out=hgs[c][:, 4 * w * r : 4 * w * (r + 1)].rearrange("p (c i t) -> p c t i", i=4, t=4),
+                    in0=hidp[c][:, :, w * r : w * (r + 1)].rearrange("p t (c i) -> p c t i", i=4),
+                    scalar1=1.0,
+                    scalar2=0.0,
+                    op0=ALU.mult,
+                    op1=ALU.add,
+                )
 
-        def st_g(c):
+        def hid_quant(c):
+            h2c[c] = work.tile([P, 512], U32, name="h2c%d" % c, tag="h2c", bufs=6, align_bytes=64)
+            h2s[c] = work.tile([P, 512], U8, name="h2s%d" % c, tag="h2s", bufs=6, align_bytes=64)
             nc.vector.quantize_mx(out=h2c[c][:].bitcast(FP8X4), scales=h2s[c][:], in_=hgs[c][:])
 
-        def st_h(c, j):
-            ps = ps_a.tile([P, 512], F32, name="ps2_%d_%d" % (c, j), tag="A")
-            ps2[(c, j)] = ps
+        def mx2(c, j, t0=0, nt=512):
+            ps = ps_m.tile([P, 512], F32, name="ps2_%d_%d_%d" % (c, j, t0), tag="M")
+            ps2[(c, j, t0)] = ps
+            w, ws = w_col(1, j)
             nc.tensor.matmul_mx(
-                out=ps[:],
-                lhsT=wcod[1][:, 128 * j : 128 * j + 128].bitcast(FP8X4),
-                lhsT_scale=wscl[1][:, 128 * j : 128 * j + 128],
-                rhs=h2c[c][:].bitcast(FP8X4),
-                rhs_scale=h2s[c][:],
+                out=ps[:, 0:nt],
+                lhsT=w,
+                lhsT_scale=ws,
+                rhs=h2c[c][:, t0 : t0 + nt].bitcast(FP8X4),
+                rhs_scale=h2s[c][:, t0 : t0 + nt],
                 start=True,
                 stop=True,
             )
 
-        def st_i(c, j):
-            if j == 0:
+        def tanh(c, j, t0=0, nt=512):
+            if j == 0 and t0 == 0:
                 fts[c] = work.tile([P, 4, 512], F32, name="ft%d" % c, tag="ft")
             nc.scalar.activation(
-                out=fts[c][:, j, :], in_=ps2[(c, j)][:], func=ACT.Sigmoid, bias=bias_sb[:, 4 + j : 5 + j], scale=1.0
+                out=fts[c][:, j, t0 : t0 + nt],
+                in_=ps2[(c, j, t0)][:, 0:nt],
+                func=ACT.Tanh if c < N_TANH else ACT.Sigmoid,
+                bias=bias_sb[:, 8 + j : 9 + j] if c < N_TANH else bias_sb[:, 4 + j : 5 + j],
+                scale=0.5 if c < N_TANH else 1.0,
             )
 
-        def st_j(c, a):
-            fb = ps_b.tile([P, 512], F32, name="fb%d_%d" % (c, a), tag="B")
-            fbs[(c, a)] = fb
+        def t_transpose(c, a):
+            for x in (a, a + 1):
+                fbs[(c, x)] = ps_t.tile([P, 512], F32, name="fb%d_%d" % (c, x), tag="T")
             for j in range(4):
-                nc.tensor.transpose(fb[:, 128 * j : 128 * j + 128], fts[c][:, j, 128 * a : 128 * a + 128], ident[:])
+                for x in (a, a + 1):
+                    nc.tensor.transpose(
+                        fbs[(c, x)][:, 128 * j : 128 * j + 128], fts[c][:, j, 128 * x : 128 * x + 128], ident[:]
+                    )
 
-        def st_k(c, a):
-            if a == 0:
+        def halve(c):
+            nc.vector.tensor_scalar_mul(out=lg_sb[c][:], in0=lg_sb[c][:], scalar1=0.5)
+
+        def product(c, a, c0=0, n=512):
+            if a == 0 and c0 == 0:
                 osb[c] = work.tile([P, 4, 512], F32, name="osb%d" % c, tag="osb")
             nc.vector.scalar_tensor_tensor(
-                out=osb[c][:, a, :],
-                in0=fbs[(c, a)][:],
-                scalar=1.0,
-                in1=lg_sb[c][:, 512 * a : 512 * a + 512],
+                out=osb[c][:, a, c0 : c0 + n],
+                in0=fbs[(c, a)][:, c0 : c0 + n],
+                scalar=3.0 if c < N_TANH else 1.0,
+                in1=lg_sb[c][:, 512 * a + c0 : 512 * a + c0 + n],
                 op0=ALU.add,
                 op1=ALU.mult,
             )
 
-        def ok(c):
-            return 0 <= c < NCH
+        def store(c, a, na):
+            nc.sync.dma_start(out=ov[:, TPC * c + a : TPC * c + a + na, :], in_=osb[c][:, a : a + na, :])
 
-        fg_slot = {1: [0], 2: [1], 4: [2], 6: [3], 7: [4, 5], 8: [6, 7]}
-        for i in range(-3, NCH + 1):
-            if i == 7:
-                for j in range(4):
-                    st_h(0, j)
-            if ok(i + 3):
-                st_a(i + 3)
-            if i == -3:
-                w_regroup(0)
-                nc.vector.tensor_copy(out=bf32[:], in_=braw[:])
-                nc.tensor.transpose(bps[:], bf32[:], ident[:])
-                w_quant(0)
-            if ok(i + 2):
-                st_b(i + 2)
-            fg = fg_slot.get(i, [])
-            for c in fg:
-                st_f(c)
-            if i == 0:
-                w_regroup(1)
-            if ok(i + 2):
-                st_c(i + 2)
-            if i == -2:
-                nc.vector.tensor_copy(out=bias_sb[:], in_=bps[:, 0:8])
-            for c in fg:
-                st_g(c)
-            if i == 0:
-                w_quant(1)
-            for m in range(4):
-                if ok(i):
-                    st_e(i, m)
-                if ok(i + 1):
-                    st_d(i + 1, m)
+        h_transpose(0, 0)
+        nc.vector.tensor_copy(out=bf32[:], in_=braw[:])
+        bps = ps_t.tile([P, P], F32, name="bps", tag="T")
+        nc.tensor.transpose(bps[:], bf32[:], ident[:])
+        h_transpose(0, 1)
+        w_regroup(0, 1, 1)
+        h_evac(0, 0, False)
+        nc.vector.tensor_copy(out=bias_sb[:, 0:8], in_=bps[:, 0:8])
+        nc.vector.tensor_scalar_mul(out=bias_sb[:, 8:12], in0=bps[:, 4:8], scalar1=0.5)
+        w_regroup(0, 0, 0)
+        h_quant(0, 0, 256)
+        w_quant(0, 0)
+        h_evac(0, 1, True)
+        w_quant(0, 1)
+        h_quant(0, 256, 256)
+        for c in (6, 7):
+            load_h(c)
+        for c in range(NCH):
+            load_lg(c)
+        done = set()
+        slot = {"M": [], "T": []}
+        for m in range(4):
+            mx1(0, m, 0, 256)
+            gelu(0, m, 0, 256)
 
-        for i in range(0, NCH + 1):
-            c = i - 1
-            if ok(c):
-                for a in range(TPC):
-                    st_j(c, a)
-                    st_k(c, a)
-                    if c == NCH - 1:
-                        nc.sync.dma_start(out=ov[:, TPC * c + a, :], in_=osb[c][:, a, :])
-                    elif a % 2 == 1:
-                        nc.sync.dma_start(out=ov[:, TPC * c + a - 1 : TPC * c + a + 1, :], in_=osb[c][:, a - 1 : a + 1, :])
+        progs = {"S": [], "E": [], "V": [], "G": []}
+
+        def put(eng, name, needs, *calls):
+            progs[eng].append((name, needs, calls))
+
+        def ring(kind, freed_by):
+            slot[kind].append(freed_by)
+            n = len(slot[kind])
+            return [slot[kind][n - 5]] if n > 4 else []
+
+        m_users = ["done"] * 4
+        for tok in S_PROG.split():
+            c = int(tok[1])
+            if tok[0] == "e":
+                b = int(tok[2])
+                put("S", "e%d%d" % (c, b), ["h%d%d" % (c, b)], (h_evac, c, b, True))
             for j in range(4):
-                if ok(i):
-                    st_i(i, j)
-                if ok(i + 1):
-                    st_h(i + 1, j)
+                if tok[0] == "g":
+                    put("S", "g%d%d" % (c, j), ["M%d%d" % (c, j)], (gelu, c, j))
+                elif tok[0] == "t":
+                    hf = tok[2:]
+                    need = ["X%d%d%s" % (c, j, hf)]
+                    if c >= 3:
+                        need.append("O%d3" % (c - 3))
+                    if hf:
+                        put("S", "t%d%d%s" % (c, j, hf), need, (tanh, c, j, 256 * (hf == "b"), 256))
+                    else:
+                        put("S", "t%d%d" % (c, j), need, (tanh, c, j))
+        for j in range(4):
+            progs["S"].insert(j, ("g0%db" % j, ["M0%db" % j], ((gelu, 0, j, 256, 256),)))
+        for tok in PE_PROG.split():
+            c = int(tok[1])
+            hf = tok[2:]
+            if tok[0] == "h":
+                for b in range(2):
+                    put("E", "h%d%d" % (c, b), ring("T", "e%d%d" % (c, b)), (h_transpose, c, b))
+            elif tok[0] == "o":
+                for g in {"a": (0,), "b": (1,)}.get(hf, (0, 1)):
+                    last = "t%d3" % c + ("ab"[g] if c == NCH - 1 else "")
+                    need = [last] + ring("T", "p%d%d" % (c, 2 * g)) + ring("T", "p%d%d" % (c, 2 * g + 1))
+                    put("E", "o%d%d" % (c, g), need, (t_transpose, c, 2 * g))
+                    put("E", "O%d%d" % (c, 2 * g + 1), [], ())
+            elif tok[0] == "M":
+                for m in range(4):
+                    if hf:
+                        put("E", "M%d%d%s" % (c, m, hf), ["q0b"] + ring("M", "g%d%d%s" % (c, m, hf)), (mx1, c, m, 256, 256))
+                    else:
+                        put("E", "M%d%d" % (c, m), ["q%d" % c] + ring("M", "g%d%d" % (c, m)), (mx1, c, m))
+            else:
+                for j in range(4):
+                    need = ["k%d" % c, "W"] + ring("M", "t%d%d%s" % (c, j, hf))
+                    if hf:
+                        put("E", "X%d%d%s" % (c, j, hf), need, (mx2, c, j, 256 * (hf == "b"), 256))
+                    else:
+                        put("E", "X%d%d" % (c, j), need, (mx2, c, j))
+        for tok in V_PROG.split():
+            if tok == "w":
+                put("V", "w", [], (w_regroup, 1, 0, W2_ENG), (w_regroup, 1, 1, W2_ENG))
+                continue
+            if tok == "W":
+                put("V", "W", ["w"], (w_quant, 1, 0), (w_quant, 1, 1))
+                continue
+            c = int(tok[1])
+            hf = tok[2:]
+            if tok[0] == "e":
+                for b in (int(hf),) if hf else (0, 1):
+                    put("V", "e%d%d" % (c, b), ["h%d%d" % (c, b)], (h_evac, c, b, False))
+            elif tok[0] == "q":
+                put("V", "q%d" % c, ["e%d0" % c, "e%d1" % c] + (["M%d3" % (c - 4)] if c > 4 else []), (h_quant, c))
+            elif tok[0] == "r":
+                put("V", "r%d" % c, ["g%d3" % c + ("b" if c == 0 else "")], (hid_regroup, c, True))
+            elif tok[0] == "k":
+                put("V", "k%d" % c, ["r%d" % c], (hid_quant, c))
+            elif tok[0] == "H":
+                put("V", "H%d" % c, [], (halve, c))
+            else:
+                for g in {"a": (0,), "b": (1,)}.get(hf, (0, 1)):
+                    for a in (2 * g, 2 * g + 1):
+                        need = ["o%d%d" % (c, g)] + (["H%d" % c] if c < N_TANH else [])
+                        if c == NCH - 1:
+                            put("V", "p%d%d" % (c, a), need, (product, c, a), (store, c, a, 1))
+                        elif a % 2 == 0:
+                            put("V", "p%d%d" % (c, a), need, (product, c, a))
+                        else:
+                            put("V", "p%d%d" % (c, a), need, (product, c, a), (store, c, 2 * g, 2))
+        for tok in G_PROG.split():
+            c = int(tok[1])
+            put("G", "r%d" % c, ["g%d3" % c + ("b" if c == 0 else "")] + (["k%d" % (c - 5)] if c > 4 else []), (hid_regroup, c, False))
+
+        done = set(["q0b"])
+        left = sum(len(p) for p in progs.values())
+        pos = {e: 0 for e in progs}
+        while left:
+            moved = False
+            for e in ("E", "S", "V", "G"):
+                while pos[e] < len(progs[e]):
+                    name, needs, calls = progs[e][pos[e]]
+                    if not all(n in done for n in needs):
+                        break
+                    for call in calls:
+                        if call:
+                            call[0](*call[1:])
+                    done.add(name)
+                    pos[e] += 1
+                    left -= 1
+                    moved = True
+                    if e == "E":
+                        break
+            assert moved, [(e, progs[e][pos[e]][:2]) for e in progs if pos[e] < len(progs[e])]

@@ -17,14 +17,50 @@ P = 128
 NCH = 8
 TPC = 4
 
-N_TANH = 1
 R_PIECES = 4
 W2_PIECES = 2
 W2_ENG = 0
-S_PROG = "e20 e21 g1 g2 g3 g4 g5 g6 g7 t0 t1 t2 t3 t4 t5 t6 t7a t7b"
-PE_PROG = "h1 M0b h2 M1 h3 M2 h4 M3 h5 M4 h6 M5 h7 M6 M7 X0 X1 o0 X2 o1 X3 o2 X4 o3 X5 o4 X6 o5 X7a o6 X7b o7a o7b"
-V_PROG = "e1 q1 w q2 W e3 q3 e4 q4 e5 q5 e6 q6 e7 q7 k0 k1 r2 r3 H0 r4 k2 k3 p0 k4 p1 k5 p2 k6 p3 k7 p4 p5 p6 p7a p7b"
-G_PROG = "r0 r1 r5 r6 r7"
+N_TANH = 5
+LAG = 3
+SCALAR_EVAC = ((2, 0), (2, 1), (3, 0))
+VECTOR_REGROUP = (0, 1)
+
+
+def build_lists():
+    sc, te, ve, gp = [], ["h1", "M0b"], [], []
+    for s in range(NCH + LAG + 1):
+        x = s - LAG
+        f = x - 1
+        sc += ["e%d%d" % cb for cb in SCALAR_EVAC if cb[0] == s + 1]
+        if 1 <= s < NCH:
+            sc.append("g%d" % s)
+        if 0 <= x < NCH:
+            sc += ["t7a", "t7b"] if x == 7 else ["t%d" % x]
+        if 1 <= s < NCH:
+            te += ["h%d" % (s + 1)] if s + 1 < NCH else []
+            te.append("M%d" % s)
+        if 0 <= x < NCH - 1:
+            te.append("X%d" % x)
+        if 0 <= f < NCH - 2:
+            te.append("o%d" % f)
+        if s + 1 < NCH:
+            banks = [b for b in range(2) if (s + 1, b) not in SCALAR_EVAC]
+            ve += ["e%d" % (s + 1)] if len(banks) == 2 else ["e%d%d" % (s + 1, b) for b in banks]
+        if s - 1 in VECTOR_REGROUP:
+            ve.append("r%d" % (s - 1))
+        if s + 1 < NCH:
+            ve.append("q%d" % (s + 1))
+        ve += {1: ["w"], 2: ["W"]}.get(s, [])
+        if 0 <= x + 1 < NCH:
+            ve.append("k%d" % (x + 1))
+        if 0 <= x < N_TANH:
+            ve.append("H%d" % x)
+        if 0 <= f < NCH:
+            ve += ["p7a", "p7b"] if f == 7 else ["p%d" % f]
+        if s < NCH and s not in VECTOR_REGROUP:
+            gp.append("r%d" % s)
+    te += ["X7a", "o6", "X7b", "o7a", "o7b"]
+    return sc, te, ve, gp
 
 
 def tile_sparseoutputprojection_pb_t_kernel(tc, hidden_states, logits, W_f1, b_f1, W_f2, b_f2, out):
@@ -36,8 +72,7 @@ def tile_sparseoutputprojection_pb_t_kernel(tc, hidden_states, logits, W_f1, b_f
     with ExitStack() as ctx:
         consts = ctx.enter_context(tc.tile_pool(name="consts", bufs=1))
         work = ctx.enter_context(tc.tile_pool(name="work", bufs=3))
-        ps_m = ctx.enter_context(tc.psum_pool(name="psm", bufs=4))
-        ps_t = ctx.enter_context(tc.psum_pool(name="pst", bufs=4))
+        ps = ctx.enter_context(tc.psum_pool(name="ps", bufs=8))
         ctx.enter_context(tc.manual_schedule())
 
         ident = consts.tile([P, P], F32, name="ident")
@@ -141,7 +176,7 @@ def tile_sparseoutputprojection_pb_t_kernel(tc, hidden_states, logits, W_f1, b_f
 
         def h_transpose(c, b):
             hw = h_sb[c][:].bitcast(F32)
-            xt = ps_t.tile([P, 2, 256], F32, name="xt%d_%d" % (c, b), tag="T")
+            xt = ps.tile([P, 2, 256], F32, name="xt%d_%d" % (c, b), tag="B")
             xts[(c, b)] = xt
             for a2 in range(2):
                 for u in range(2):
@@ -169,11 +204,11 @@ def tile_sparseoutputprojection_pb_t_kernel(tc, hidden_states, logits, W_f1, b_f
             )
 
         def mx1(c, m, t0=0, nt=512):
-            ps = ps_m.tile([P, 512], F32, name="ps1_%d_%d_%d" % (c, m, t0), tag="M")
-            ps1[(c, m, t0)] = ps
+            pt = ps.tile([P, 512], F32, name="ps1_%d_%d_%d" % (c, m, t0), tag="B")
+            ps1[(c, m, t0)] = pt
             w, ws = w_col(0, m)
             nc.tensor.matmul_mx(
-                out=ps[:, 0:nt],
+                out=pt[:, 0:nt],
                 lhsT=w,
                 lhsT_scale=ws,
                 rhs=hcs[c][:, t0 : t0 + nt].bitcast(FP8X4),
@@ -218,11 +253,11 @@ def tile_sparseoutputprojection_pb_t_kernel(tc, hidden_states, logits, W_f1, b_f
             nc.vector.quantize_mx(out=h2c[c][:].bitcast(FP8X4), scales=h2s[c][:], in_=hgs[c][:])
 
         def mx2(c, j, t0=0, nt=512):
-            ps = ps_m.tile([P, 512], F32, name="ps2_%d_%d_%d" % (c, j, t0), tag="M")
-            ps2[(c, j, t0)] = ps
+            pt = ps.tile([P, 512], F32, name="ps2_%d_%d_%d" % (c, j, t0), tag="B")
+            ps2[(c, j, t0)] = pt
             w, ws = w_col(1, j)
             nc.tensor.matmul_mx(
-                out=ps[:, 0:nt],
+                out=pt[:, 0:nt],
                 lhsT=w,
                 lhsT_scale=ws,
                 rhs=h2c[c][:, t0 : t0 + nt].bitcast(FP8X4),
@@ -244,7 +279,7 @@ def tile_sparseoutputprojection_pb_t_kernel(tc, hidden_states, logits, W_f1, b_f
 
         def t_transpose(c, a):
             for x in (a, a + 1):
-                fbs[(c, x)] = ps_t.tile([P, 512], F32, name="fb%d_%d" % (c, x), tag="T")
+                fbs[(c, x)] = ps.tile([P, 512], F32, name="fb%d_%d" % (c, x), tag="B")
             for j in range(4):
                 for x in (a, a + 1):
                     nc.tensor.transpose(
@@ -271,7 +306,7 @@ def tile_sparseoutputprojection_pb_t_kernel(tc, hidden_states, logits, W_f1, b_f
 
         h_transpose(0, 0)
         nc.vector.tensor_copy(out=bf32[:], in_=braw[:])
-        bps = ps_t.tile([P, P], F32, name="bps", tag="T")
+        bps = ps.tile([P, P], F32, name="bps", tag="B")
         nc.tensor.transpose(bps[:], bf32[:], ident[:])
         h_transpose(0, 1)
         w_regroup(0, 1, 1)
@@ -289,23 +324,23 @@ def tile_sparseoutputprojection_pb_t_kernel(tc, hidden_states, logits, W_f1, b_f
         for c in range(NCH):
             load_lg(c)
         done = set()
-        slot = {"M": [], "T": []}
+        slot = ["done"] * 7
         for m in range(4):
             mx1(0, m, 0, 256)
             gelu(0, m, 0, 256)
 
+        S_PROG, PE_PROG, V_PROG, G_PROG = build_lists()
         progs = {"S": [], "E": [], "V": [], "G": []}
 
         def put(eng, name, needs, *calls):
             progs[eng].append((name, needs, calls))
 
         def ring(kind, freed_by):
-            slot[kind].append(freed_by)
-            n = len(slot[kind])
-            return [slot[kind][n - 5]] if n > 4 else []
+            slot.append(freed_by)
+            n = len(slot)
+            return [slot[n - 9]] if n > 8 else []
 
-        m_users = ["done"] * 4
-        for tok in S_PROG.split():
+        for tok in S_PROG:
             c = int(tok[1])
             if tok[0] == "e":
                 b = int(tok[2])
@@ -324,7 +359,7 @@ def tile_sparseoutputprojection_pb_t_kernel(tc, hidden_states, logits, W_f1, b_f
                         put("S", "t%d%d" % (c, j), need, (tanh, c, j))
         for j in range(4):
             progs["S"].insert(j, ("g0%db" % j, ["M0%db" % j], ((gelu, 0, j, 256, 256),)))
-        for tok in PE_PROG.split():
+        for tok in PE_PROG:
             c = int(tok[1])
             hf = tok[2:]
             if tok[0] == "h":
@@ -343,13 +378,15 @@ def tile_sparseoutputprojection_pb_t_kernel(tc, hidden_states, logits, W_f1, b_f
                     else:
                         put("E", "M%d%d" % (c, m), ["q%d" % c] + ring("M", "g%d%d" % (c, m)), (mx1, c, m))
             else:
-                for j in range(4):
+                js = {"l": (0, 1), "h": (2, 3)}.get(hf, (0, 1, 2, 3))
+                hf = "" if hf in ("l", "h") else hf
+                for j in js:
                     need = ["k%d" % c, "W"] + ring("M", "t%d%d%s" % (c, j, hf))
                     if hf:
                         put("E", "X%d%d%s" % (c, j, hf), need, (mx2, c, j, 256 * (hf == "b"), 256))
                     else:
                         put("E", "X%d%d" % (c, j), need, (mx2, c, j))
-        for tok in V_PROG.split():
+        for tok in V_PROG:
             if tok == "w":
                 put("V", "w", [], (w_regroup, 1, 0, W2_ENG), (w_regroup, 1, 1, W2_ENG))
                 continue
@@ -379,11 +416,11 @@ def tile_sparseoutputprojection_pb_t_kernel(tc, hidden_states, logits, W_f1, b_f
                             put("V", "p%d%d" % (c, a), need, (product, c, a))
                         else:
                             put("V", "p%d%d" % (c, a), need, (product, c, a), (store, c, 2 * g, 2))
-        for tok in G_PROG.split():
+        for tok in G_PROG:
             c = int(tok[1])
             put("G", "r%d" % c, ["g%d3" % c + ("b" if c == 0 else "")] + (["k%d" % (c - 5)] if c > 4 else []), (hid_regroup, c, False))
 
-        done = set(["q0b"])
+        done = set(["q0b", "done"])
         left = sum(len(p) for p in progs.values())
         pos = {e: 0 for e in progs}
         while left:

from contextlib import ExitStack

import concourse.mybir as mybir
from concourse.masks import make_identity

FLOPS = 2 * 4096 * 512 * 512 * 2

BF16 = mybir.dt.bfloat16
F32 = mybir.dt.float32
U32 = mybir.dt.uint32
U8 = mybir.dt.uint8
FP8X4 = mybir.dt.float8_e4m3fn_x4
ACT = mybir.ActivationFunctionType
ALU = mybir.AluOpType

P = 128
NCH = 8
TPC = 4

R_PIECES = 4
W2_PIECES = 2
W2_ENG = 0
N_TANH = 5
LAG = 3
SCALAR_EVAC = ((2, 0), (2, 1), (3, 0))
VECTOR_REGROUP = (0, 1)


def build_lists():
    sc, te, ve, gp = [], ["h1", "M0b"], [], []
    for s in range(NCH + LAG + 1):
        x = s - LAG
        f = x - 1
        sc += ["e%d%d" % cb for cb in SCALAR_EVAC if cb[0] == s + 1]
        if 1 <= s < NCH:
            sc.append("g%d" % s)
        if 0 <= x < NCH:
            sc += ["t7a", "t7b"] if x == 7 else ["t%d" % x]
        if 1 <= s < NCH:
            te += ["h%d" % (s + 1)] if s + 1 < NCH else []
            te.append("M%d" % s)
        if 0 <= x < NCH - 1:
            te.append("X%d" % x)
        if 0 <= f < NCH - 2:
            te.append("o%d" % f)
        if s + 1 < NCH:
            banks = [b for b in range(2) if (s + 1, b) not in SCALAR_EVAC]
            ve += ["e%d" % (s + 1)] if len(banks) == 2 else ["e%d%d" % (s + 1, b) for b in banks]
        if s - 1 in VECTOR_REGROUP:
            ve.append("r%d" % (s - 1))
        if s + 1 < NCH:
            ve.append("q%d" % (s + 1))
        ve += {1: ["w"], 2: ["W"]}.get(s, [])
        if 0 <= x + 1 < NCH:
            ve.append("k%d" % (x + 1))
        if 0 <= x < N_TANH:
            ve.append("H%d" % x)
        if 0 <= f < NCH:
            ve += ["p7a", "p7b"] if f == 7 else ["p%d" % f]
        if s < NCH and s not in VECTOR_REGROUP:
            gp.append("r%d" % s)
    te += ["X7a", "o6", "X7b", "o7a", "o7b"]
    return sc, te, ve, gp


def tile_sparseoutputprojection_pb_t_kernel(tc, hidden_states, logits, W_f1, b_f1, W_f2, b_f2, out):
    nc = tc.nc
    hv = hidden_states.flatten_outer_dims().rearrange("(p n) d -> p n d", n=32)
    lv = logits.flatten_outer_dims().rearrange("(p n) d -> p n d", n=32)
    ov = out.flatten_outer_dims().rearrange("(p n) d -> p n d", n=32)

    with ExitStack() as ctx:
        consts = ctx.enter_context(tc.tile_pool(name="consts", bufs=1))
        work = ctx.enter_context(tc.tile_pool(name="work", bufs=3))
        ps = ctx.enter_context(tc.psum_pool(name="ps", bufs=8))
        ctx.enter_context(tc.manual_schedule())

        ident = consts.tile([P, P], F32, name="ident")
        warm = consts.tile([P, 1], F32, name="warm")
        warm2 = consts.tile([P, 1], F32, name="warm2")
        braw = consts.tile([P, P], BF16, name="braw")
        bf32 = consts.tile([P, P], F32, name="bf32")
        bias_sb = consts.tile([P, 12], F32, name="bias_sb")
        wraw = {}
        wgrp = {}
        wcod = {}
        wscl = {}
        for s in range(2):
            wraw[s] = consts.tile([P, 4, 512], BF16, name="wraw%d" % s)
            for hf in range(2):
                wgrp[(s, hf)] = consts.tile([P, 1024], BF16, name="wgrp%d_%d" % (s, hf), align_bytes=64)
                wcod[(s, hf)] = consts.tile([P, 256], U32, name="wcod%d_%d" % (s, hf), align_bytes=64)
                wscl[(s, hf)] = consts.tile([P, 256], U8, name="wscl%d_%d" % (s, hf), align_bytes=64)
        h_sb = {}
        lg_sb = {}
        for c in range(NCH):
            lg_sb[c] = consts.tile([P, 2048], BF16, name="lg_sb%d" % c)

        nc.vector.memset(warm[:], 0.0)
        nc.vector.memset(braw[:], 0.0)
        nc.scalar.activation(out=warm2[:], in_=warm[:], func=ACT.Gelu)
        make_identity(nc, ident[:])

        def load_h(c, n0=0, nn=TPC):
            if n0 == 0:
                h_sb[c] = work.tile([P, 2048], BF16, name="h_sb%d" % c, tag="h_sb", bufs=7)
            nc.sync.dma_start(
                out=h_sb[c][:, 512 * n0 : 512 * (n0 + nn)].rearrange("p (n d) -> p n d", n=nn),
                in_=hv[:, TPC * c + n0 : TPC * c + n0 + nn, :],
            )

        def load_lg(c):
            nc.sync.dma_start(
                out=lg_sb[c][:].rearrange("p (n d) -> p n d", n=TPC),
                in_=lv[:, TPC * c : TPC * c + TPC, :],
            )

        def load_w1(u):
            nc.sync.dma_start(
                out=wraw[0][:, 2 * u : 2 * u + 2, :],
                in_=W_f1[256 * u : 256 * u + 256, :].rearrange("(q e) c -> q e c", e=2),
            )

        load_h(0, 0, 2)
        nc.sync.dma_start(out=braw[0:4, :], in_=b_f1.rearrange("(t p) -> t p", p=P))
        nc.sync.dma_start(out=braw[4:8, :], in_=b_f2.rearrange("(t p) -> t p", p=P))
        load_w1(0)
        load_w1(1)
        load_h(0, 2, 2)
        load_h(1)
        load_h(2)
        nc.sync.dma_start(out=wraw[1][:], in_=W_f2.rearrange("(t p) v -> p t v", p=P))
        load_h(3)
        load_h(4)
        load_h(5)

        def w_regroup(s, hf, eng):
            dst = wgrp[(s, hf)][:].rearrange("p (c i t) -> p c t i", i=4, t=4)
            src = wraw[s][:, :, 256 * hf : 256 * hf + 256].rearrange("p t (c i) -> p c t i", i=4)
            if eng == 0:
                nc.vector.tensor_copy(out=dst, in_=src)
            elif eng == 1:
                nc.scalar.copy(out=dst, in_=src)
            else:
                w = 256 // W2_PIECES
                for r in range(W2_PIECES):
                    nc.gpsimd.tensor_scalar(
                        out=wgrp[(s, hf)][:, 4 * w * r : 4 * w * (r + 1)].rearrange("p (c i t) -> p c t i", i=4, t=4),
                        in0=wraw[s][:, :, 256 * hf + w * r : 256 * hf + w * (r + 1)].rearrange("p t (c i) -> p c t i", i=4),
                        scalar1=1.0,
                        scalar2=0.0,
                        op0=ALU.mult,
                        op1=ALU.add,
                    )

        def w_quant(s, hf):
            nc.vector.quantize_mx(out=wcod[(s, hf)][:].bitcast(FP8X4), scales=wscl[(s, hf)][:], in_=wgrp[(s, hf)][:])

        def w_col(s, m):
            lo = 128 * (m % 2)
            return wcod[(s, m // 2)][:, lo : lo + 128].bitcast(FP8X4), wscl[(s, m // 2)][:, lo : lo + 128]

        xts = {}
        grps = {}
        hcs = {}
        hss = {}
        ps1 = {}
        hidp = {}
        hgs = {}
        h2c = {}
        h2s = {}
        ps2 = {}
        fts = {}
        fbs = {}
        osb = {}

        def h_transpose(c, b):
            hw = h_sb[c][:].bitcast(F32)
            xt = ps.tile([P, 2, 256], F32, name="xt%d_%d" % (c, b), tag="B")
            xts[(c, b)] = xt
            for a2 in range(2):
                for u in range(2):
                    col = 256 * (2 * b + a2) + 128 * u
                    nc.tensor.transpose(xt[:, u, 128 * a2 : 128 * a2 + 128], hw[:, col : col + 128], ident[:])

        def h_evac(c, b, scalar):
            if b == 0:
                grps[c] = work.tile([P, 2048], BF16, name="grp%d" % c, tag="grp", bufs=3, align_bytes=64)
            dst = grps[c][:].bitcast(F32)[:, 512 * b : 512 * b + 512].rearrange("p (n u) -> p n u", u=2)
            src = xts[(c, b)][:].rearrange("p u n -> p n u")
            if scalar:
                nc.scalar.copy(out=dst, in_=src)
            else:
                nc.vector.tensor_copy(out=dst, in_=src)

        def h_quant(c, t0=0, nt=512):
            if t0 == 0:
                hcs[c] = work.tile([P, 512], U32, name="hc%d" % c, tag="hc", bufs=4, align_bytes=64)
                hss[c] = work.tile([P, 512], U8, name="hs%d" % c, tag="hs", bufs=4, align_bytes=64)
            nc.vector.quantize_mx(
                out=hcs[c][:, t0 : t0 + nt].bitcast(FP8X4),
                scales=hss[c][:, t0 : t0 + nt],
                in_=grps[c][:, 4 * t0 : 4 * t0 + 4 * nt],
            )

        def mx1(c, m, t0=0, nt=512):
            pt = ps.tile([P, 512], F32, name="ps1_%d_%d_%d" % (c, m, t0), tag="B")
            ps1[(c, m, t0)] = pt
            w, ws = w_col(0, m)
            nc.tensor.matmul_mx(
                out=pt[:, 0:nt],
                lhsT=w,
                lhsT_scale=ws,
                rhs=hcs[c][:, t0 : t0 + nt].bitcast(FP8X4),
                rhs_scale=hss[c][:, t0 : t0 + nt],
                start=True,
                stop=True,
            )

        def gelu(c, m, t0=0, nt=512):
            if m == 0 and t0 == 0:
                hidp[c] = work.tile([P, 4, 512], BF16, name="hidp%d" % c, tag="hidp", bufs=7)
            nc.scalar.activation(
                out=hidp[c][:, m, t0 : t0 + nt],
                in_=ps1[(c, m, t0)][:, 0:nt],
                func=ACT.Gelu,
                bias=bias_sb[:, m : m + 1],
                scale=1.0,
            )

        def hid_regroup(c, vec):
            hgs[c] = work.tile([P, 2048], BF16, name="hg%d" % c, tag="hg", bufs=6, align_bytes=64)
            if vec:
                nc.vector.tensor_copy(
                    out=hgs[c][:].rearrange("p (c i t) -> p c t i", i=4, t=4),
                    in_=hidp[c][:].rearrange("p t (c i) -> p c t i", i=4),
                )
                return
            w = 512 // R_PIECES
            for r in range(R_PIECES):
                nc.gpsimd.tensor_scalar(
                    out=hgs[c][:, 4 * w * r : 4 * w * (r + 1)].rearrange("p (c i t) -> p c t i", i=4, t=4),
                    in0=hidp[c][:, :, w * r : w * (r + 1)].rearrange("p t (c i) -> p c t i", i=4),
                    scalar1=1.0,
                    scalar2=0.0,
                    op0=ALU.mult,
                    op1=ALU.add,
                )

        def hid_quant(c):
            h2c[c] = work.tile([P, 512], U32, name="h2c%d" % c, tag="h2c", bufs=6, align_bytes=64)
            h2s[c] = work.tile([P, 512], U8, name="h2s%d" % c, tag="h2s", bufs=6, align_bytes=64)
            nc.vector.quantize_mx(out=h2c[c][:].bitcast(FP8X4), scales=h2s[c][:], in_=hgs[c][:])

        def mx2(c, j, t0=0, nt=512):
            pt = ps.tile([P, 512], F32, name="ps2_%d_%d_%d" % (c, j, t0), tag="B")
            ps2[(c, j, t0)] = pt
            w, ws = w_col(1, j)
            nc.tensor.matmul_mx(
                out=pt[:, 0:nt],
                lhsT=w,
                lhsT_scale=ws,
                rhs=h2c[c][:, t0 : t0 + nt].bitcast(FP8X4),
                rhs_scale=h2s[c][:, t0 : t0 + nt],
                start=True,
                stop=True,
            )

        def tanh(c, j, t0=0, nt=512):
            if j == 0 and t0 == 0:
                fts[c] = work.tile([P, 4, 512], F32, name="ft%d" % c, tag="ft")
            nc.scalar.activation(
                out=fts[c][:, j, t0 : t0 + nt],
                in_=ps2[(c, j, t0)][:, 0:nt],
                func=ACT.Tanh if c < N_TANH else ACT.Sigmoid,
                bias=bias_sb[:, 8 + j : 9 + j] if c < N_TANH else bias_sb[:, 4 + j : 5 + j],
                scale=0.5 if c < N_TANH else 1.0,
            )

        def t_transpose(c, a):
            for x in (a, a + 1):
                fbs[(c, x)] = ps.tile([P, 512], F32, name="fb%d_%d" % (c, x), tag="B")
            for j in range(4):
                for x in (a, a + 1):
                    nc.tensor.transpose(
                        fbs[(c, x)][:, 128 * j : 128 * j + 128], fts[c][:, j, 128 * x : 128 * x + 128], ident[:]
                    )

        def halve(c):
            nc.vector.tensor_scalar_mul(out=lg_sb[c][:], in0=lg_sb[c][:], scalar1=0.5)

        def product(c, a, c0=0, n=512):
            if a == 0 and c0 == 0:
                osb[c] = work.tile([P, 4, 512], F32, name="osb%d" % c, tag="osb")
            nc.vector.scalar_tensor_tensor(
                out=osb[c][:, a, c0 : c0 + n],
                in0=fbs[(c, a)][:, c0 : c0 + n],
                scalar=3.0 if c < N_TANH else 1.0,
                in1=lg_sb[c][:, 512 * a + c0 : 512 * a + c0 + n],
                op0=ALU.add,
                op1=ALU.mult,
            )

        def store(c, a, na):
            nc.sync.dma_start(out=ov[:, TPC * c + a : TPC * c + a + na, :], in_=osb[c][:, a : a + na, :])

        h_transpose(0, 0)
        nc.vector.tensor_copy(out=bf32[:], in_=braw[:])
        bps = ps.tile([P, P], F32, name="bps", tag="B")
        nc.tensor.transpose(bps[:], bf32[:], ident[:])
        h_transpose(0, 1)
        w_regroup(0, 1, 1)
        h_evac(0, 0, False)
        nc.vector.tensor_copy(out=bias_sb[:, 0:8], in_=bps[:, 0:8])
        nc.vector.tensor_scalar_mul(out=bias_sb[:, 8:12], in0=bps[:, 4:8], scalar1=0.5)
        w_regroup(0, 0, 0)
        h_quant(0, 0, 256)
        w_quant(0, 0)
        h_evac(0, 1, True)
        w_quant(0, 1)
        h_quant(0, 256, 256)
        for c in (6, 7):
            load_h(c)
        for c in range(NCH):
            load_lg(c)
        done = set()
        slot = ["done"] * 7
        for m in range(4):
            mx1(0, m, 0, 256)
            gelu(0, m, 0, 256)

        S_PROG, PE_PROG, V_PROG, G_PROG = build_lists()
        progs = {"S": [], "E": [], "V": [], "G": []}

        def put(eng, name, needs, *calls):
            progs[eng].append((name, needs, calls))

        def ring(kind, freed_by):
            slot.append(freed_by)
            n = len(slot)
            return [slot[n - 9]] if n > 8 else []

        for tok in S_PROG:
            c = int(tok[1])
            if tok[0] == "e":
                b = int(tok[2])
                put("S", "e%d%d" % (c, b), ["h%d%d" % (c, b)], (h_evac, c, b, True))
            for j in range(4):
                if tok[0] == "g":
                    put("S", "g%d%d" % (c, j), ["M%d%d" % (c, j)], (gelu, c, j))
                elif tok[0] == "t":
                    hf = tok[2:]
                    need = ["X%d%d%s" % (c, j, hf)]
                    if c >= 3:
                        need.append("O%d3" % (c - 3))
                    if hf:
                        put("S", "t%d%d%s" % (c, j, hf), need, (tanh, c, j, 256 * (hf == "b"), 256))
                    else:
                        put("S", "t%d%d" % (c, j), need, (tanh, c, j))
        for j in range(4):
            progs["S"].insert(j, ("g0%db" % j, ["M0%db" % j], ((gelu, 0, j, 256, 256),)))
        for tok in PE_PROG:
            c = int(tok[1])
            hf = tok[2:]
            if tok[0] == "h":
                for b in range(2):
                    put("E", "h%d%d" % (c, b), ring("T", "e%d%d" % (c, b)), (h_transpose, c, b))
            elif tok[0] == "o":
                for g in {"a": (0,), "b": (1,)}.get(hf, (0, 1)):
                    last = "t%d3" % c + ("ab"[g] if c == NCH - 1 else "")
                    need = [last] + ring("T", "p%d%d" % (c, 2 * g)) + ring("T", "p%d%d" % (c, 2 * g + 1))
                    put("E", "o%d%d" % (c, g), need, (t_transpose, c, 2 * g))
                    put("E", "O%d%d" % (c, 2 * g + 1), [], ())
            elif tok[0] == "M":
                for m in range(4):
                    if hf:
                        put("E", "M%d%d%s" % (c, m, hf), ["q0b"] + ring("M", "g%d%d%s" % (c, m, hf)), (mx1, c, m, 256, 256))
                    else:
                        put("E", "M%d%d" % (c, m), ["q%d" % c] + ring("M", "g%d%d" % (c, m)), (mx1, c, m))
            else:
                js = {"l": (0, 1), "h": (2, 3)}.get(hf, (0, 1, 2, 3))
                hf = "" if hf in ("l", "h") else hf
                for j in js:
                    need = ["k%d" % c, "W"] + ring("M", "t%d%d%s" % (c, j, hf))
                    if hf:
                        put("E", "X%d%d%s" % (c, j, hf), need, (mx2, c, j, 256 * (hf == "b"), 256))
                    else:
                        put("E", "X%d%d" % (c, j), need, (mx2, c, j))
        for tok in V_PROG:
            if tok == "w":
                put("V", "w", [], (w_regroup, 1, 0, W2_ENG), (w_regroup, 1, 1, W2_ENG))
                continue
            if tok == "W":
                put("V", "W", ["w"], (w_quant, 1, 0), (w_quant, 1, 1))
                continue
            c = int(tok[1])
            hf = tok[2:]
            if tok[0] == "e":
                for b in (int(hf),) if hf else (0, 1):
                    put("V", "e%d%d" % (c, b), ["h%d%d" % (c, b)], (h_evac, c, b, False))
            elif tok[0] == "q":
                put("V", "q%d" % c, ["e%d0" % c, "e%d1" % c] + (["M%d3" % (c - 4)] if c > 4 else []), (h_quant, c))
            elif tok[0] == "r":
                put("V", "r%d" % c, ["g%d3" % c + ("b" if c == 0 else "")], (hid_regroup, c, True))
            elif tok[0] == "k":
                put("V", "k%d" % c, ["r%d" % c], (hid_quant, c))
            elif tok[0] == "H":
                put("V", "H%d" % c, [], (halve, c))
            else:
                for g in {"a": (0,), "b": (1,)}.get(hf, (0, 1)):
                    for a in (2 * g, 2 * g + 1):
                        need = ["o%d%d" % (c, g)] + (["H%d" % c] if c < N_TANH else [])
                        if c == NCH - 1:
                            put("V", "p%d%d" % (c, a), need, (product, c, a), (store, c, a, 1))
                        elif a % 2 == 0:
                            put("V", "p%d%d" % (c, a), need, (product, c, a))
                        else:
                            put("V", "p%d%d" % (c, a), need, (product, c, a), (store, c, 2 * g, 2))
        for tok in G_PROG:
            c = int(tok[1])
            put("G", "r%d" % c, ["g%d3" % c + ("b" if c == 0 else "")] + (["k%d" % (c - 5)] if c > 4 else []), (hid_regroup, c, False))

        done = set(["q0b", "done"])
        left = sum(len(p) for p in progs.values())
        pos = {e: 0 for e in progs}
        while left:
            moved = False
            for e in ("E", "S", "V", "G"):
                while pos[e] < len(progs[e]):
                    name, needs, calls = progs[e][pos[e]]
                    if not all(n in done for n in needs):
                        break
                    for call in calls:
                        if call:
                            call[0](*call[1:])
                    done.add(name)
                    pos[e] += 1
                    left -= 1
                    moved = True
                    if e == "E":
                        break
            assert moved, [(e, progs[e][pos[e]][:2]) for e in progs if pos[e] < len(progs[e])]
